import numpy as np
import ml_dtypes

BF16 = ml_dtypes.bfloat16


def bf(x):
    return np.asarray(x, np.float32).astype(BF16)


def f32(x):
    return np.asarray(x, np.float32)


def f64(x):
    return np.asarray(x).astype(np.float64)


def striped(idx):
    return np.tile(idx.reshape(-1, 16).T, (8, 1))


H, H2, H3, K, S, N, KN = 128, 256, 384, 4, 256, 128, 512


def sigmoid(v):
    return 1.0 / (1.0 + np.exp(-v))


def setup_inputs():
    return {
        "base": f32(0.5 * np.random.standard_normal((H, S))),
        "h_mail": bf(np.random.standard_normal((H, KN))),
        "c_mail": f32(np.random.standard_normal((H, KN))),
        "lab": f32(np.random.random((1, KN)) < 0.5),
        "iou_x": f32(np.random.standard_normal((H3, N))),
        "wf_x": f32(np.random.standard_normal((H, N))),
        "u_iou": bf(np.random.standard_normal((H2, H3)) / np.sqrt(K * H)),
        "u_f": bf(np.random.standard_normal((H2, H)) / np.sqrt(H)),
        "b_iou": f32(0.3 * np.random.standard_normal((H3, 1))),
        "b_f": f32(0.3 * np.random.standard_normal((H, 1))),
        "offs": striped(np.random.permutation(S)[:N]),
    }


def reference(base, h_mail, c_mail, lab, iou_x, wf_x, u_iou, u_f, b_iou, b_f, offs):
    idx = offs[:16].T.reshape(-1)
    h1 = f64(lab) * f64(h_mail)
    h0 = (1.0 - f64(lab)) * f64(h_mail)
    h_two = np.concatenate([h0, h1], axis=0)
    f_mid = f64(u_f).T @ h_two
    f = sigmoid(np.tile(f64(wf_x), (1, K)) + f_mid + f64(b_f))
    c_agg = (f * f64(c_mail)).reshape(H, K, N).sum(axis=1)
    iou = f64(iou_x) + f64(u_iou).T @ h_two.reshape(H2, K, N).sum(axis=1) + f64(b_iou)
    vi = sigmoid(iou[:H])
    vo = sigmoid(iou[H:H2])
    vu = np.tanh(iou[H2:])
    cell = vi * vu + c_agg
    out = f64(base).copy()
    out[:, idx] = vo * np.tanh(cell)
    return out

@@ -1,0 +1,107 @@
+import concourse.mybir as mybir
+
+F32 = mybir.dt.float32
+BF16 = mybir.dt.bfloat16
+U16 = mybir.dt.uint16
+ALU = mybir.AluOpType
+ACT = mybir.ActivationFunctionType
+
+H = 128
+K = 4
+N = 128
+KN = K * N
+S = 256
+GATES = 3
+
+FLOPS = 2 * (2 * H) * H * KN + 2 * (2 * H) * (GATES * H) * N
+
+
+def tile_improvedgraphlstmcell_kernel(
+    tc, base, h_mail, c_mail, lab, iou_x, wf_x, u_iou, u_f, b_iou, b_f, offs, out
+):
+    nc = tc.nc
+    with (
+        tc.tile_pool(name="held", bufs=1) as held,
+        tc.psum_pool(name="psum", bufs=1) as psum,
+    ):
+        offsets = held.tile([H, N // 16], U16, name="offsets")
+        nc.sync.dma_start(offsets[:], offs)
+
+        lab_all = held.tile([H, KN], F32, name="lab_all")
+        nc.sync.dma_start(lab_all[:], lab.rearrange("o q -> (o q)").partition_broadcast(H))
+        h_all = held.tile([H, KN], BF16, name="h_all")
+        nc.scalar.dma_start(h_all[:], h_mail)
+        uf_sb = held.tile([H, 2, H], BF16, name="uf_sb")
+        nc.scalar.dma_start(uf_sb[:], u_f.rearrange("(s d) c -> d s c", s=2))
+        uiou_sb = held.tile([H, 2, GATES * H], BF16, name="uiou_sb")
+        nc.gpsimd.dma_start(uiou_sb[:], u_iou.rearrange("(s d) r -> d s r", s=2))
+        wfx_sb = held.tile([H, N], F32, name="wfx_sb")
+        nc.scalar.dma_start(wfx_sb[:], wf_x)
+        ioux_sb = held.tile([H, GATES, N], F32, name="ioux_sb")
+        nc.gpsimd.dma_start(ioux_sb[:], iou_x.rearrange("(g c) j -> c g j", g=GATES))
+        c_all = held.tile([H, KN], F32, name="c_all")
+        nc.sync.dma_start(c_all[:], c_mail)
+        bf_sb = held.tile([H, 1], F32, name="bf_sb")
+        biou_sb = held.tile([H, GATES], F32, name="biou_sb")
+        with nc.allow_non_contiguous_dma(reason="one bias value to a partition"):
+            nc.scalar.dma_start(bf_sb[:], b_f)
+            nc.scalar.dma_start(biou_sb[:], b_iou.rearrange("(g c) o -> c (g o)", g=GATES))
+        window = held.tile([H, S], F32, name="window")
+        nc.sync.dma_start(window[:], base)
+
+        h1 = held.tile([H, KN], BF16, name="h1")
+        nc.vector.tensor_tensor(h1[:], h_all[:], lab_all[:], ALU.mult)
+        h0 = held.tile([H, KN], BF16, name="h0")
+        nc.vector.tensor_tensor(h0[:], h_all[:], h1[:], ALU.subtract)
+        halves = (h0, h1)
+
+        f_ps = psum.tile([H, KN], F32, name="f_ps")
+        for s in range(2):
+            nc.tensor.matmul(f_ps[:], uf_sb[:, s, :], halves[s][:], start=(s == 0), stop=(s == 1))
+        f_pre = held.tile([H, K, N], F32, name="f_pre")
+        nc.vector.tensor_tensor(
+            f_pre[:],
+            f_ps[:].rearrange("c (k j) -> c k j", k=K),
+            wfx_sb[:].unsqueeze(1).to_broadcast([H, K, N]),
+            ALU.add,
+        )
+        f_gate = held.tile([H, KN], F32, name="f_gate")
+        nc.scalar.activation(
+            f_gate[:], f_pre[:].rearrange("c k j -> c (k j)"), ACT.Sigmoid, bias=bf_sb[:, 0:1]
+        )
+
+        functions = (ACT.Sigmoid, ACT.Sigmoid, ACT.Tanh)
+        gates = []
+        for g in range(GATES):
+            iou_ps = psum.tile([H, N], F32, name=f"iou_ps{g}")
+            for s in range(2):
+                for k in range(K):
+                    nc.tensor.matmul(
+                        iou_ps[:],
+                        uiou_sb[:, s, g * H : (g + 1) * H],
+                        halves[s][:, k * N : (k + 1) * N],
+                        start=(s == 0 and k == 0),
+                        stop=(s == 1 and k == K - 1),
+                    )
+            iou_pre = held.tile([H, N], F32, name=f"iou_pre{g}")
+            nc.vector.tensor_tensor(iou_pre[:], iou_ps[:], ioux_sb[:, g, :], ALU.add)
+            gate = held.tile([H, N], F32, name=f"gate{g}")
+            nc.scalar.activation(gate[:], iou_pre[:], functions[g], bias=biou_sb[:, g : g + 1])
+            gates.append(gate)
+        vi, vo, vu = gates
+
+        fc = held.tile([H, KN], F32, name="fc")
+        nc.vector.tensor_tensor(fc[:], f_gate[:], c_all[:], ALU.mult)
+        fc_pairs = held.tile([H, 2 * N], F32, name="fc_pairs")
+        nc.vector.tensor_tensor(fc_pairs[:], fc[:, 0 : 2 * N], fc[:, 2 * N : 4 * N], ALU.add)
+        c_agg = held.tile([H, N], F32, name="c_agg")
+        nc.vector.tensor_tensor(c_agg[:], fc_pairs[:, 0:N], fc_pairs[:, N : 2 * N], ALU.add)
+        iu = held.tile([H, N], F32, name="iu")
+        nc.vector.tensor_tensor(iu[:], vi[:], vu[:], ALU.mult)
+        cell = held.tile([H, N], F32, name="cell")
+        nc.vector.tensor_tensor(cell[:], iu[:], c_agg[:], ALU.add)
+        tanh_cell = held.tile([H, N], F32, name="tanh_cell")
+        nc.scalar.activation(tanh_cell[:], cell[:], ACT.Tanh)
+
+        nc.vector.tensor_tensor(window[:].indirect(offsets[:]), vo[:], tanh_cell[:], ALU.mult)
+        nc.sync.dma_start(out, window[:])

@@ -11,7 +11,12 @@ K = 4
 N = 128
 KN = K * N
 S = 256
+GATE_I, GATE_O, GATE_U = 0, 1, 2
 GATES = 3
+PIECES = 2
+PK = K // PIECES
+PW = PK * N
+WARM_MATMULS = 3
 
 FLOPS = 2 * (2 * H) * H * KN + 2 * (2 * H) * (GATES * H) * N
 
@@ -24,84 +29,107 @@ def tile_improvedgraphlstmcell_kernel(
         tc.tile_pool(name="held", bufs=1) as held,
         tc.psum_pool(name="psum", bufs=1) as psum,
     ):
-        offsets = held.tile([H, N // 16], U16, name="offsets")
-        nc.sync.dma_start(offsets[:], offs)
-
-        lab_all = held.tile([H, KN], F32, name="lab_all")
-        nc.sync.dma_start(lab_all[:], lab.rearrange("o q -> (o q)").partition_broadcast(H))
-        h_all = held.tile([H, KN], BF16, name="h_all")
-        nc.scalar.dma_start(h_all[:], h_mail)
+        lab_all = [held.tile([H, PW], F32, name=f"lab_all{p}") for p in range(PIECES)]
+        h_all = [held.tile([H, PW], BF16, name=f"h_all{p}") for p in range(PIECES)]
         uf_sb = held.tile([H, 2, H], BF16, name="uf_sb")
-        nc.scalar.dma_start(uf_sb[:], u_f.rearrange("(s d) c -> d s c", s=2))
-        uiou_sb = held.tile([H, 2, GATES * H], BF16, name="uiou_sb")
-        nc.gpsimd.dma_start(uiou_sb[:], u_iou.rearrange("(s d) r -> d s r", s=2))
         wfx_sb = held.tile([H, N], F32, name="wfx_sb")
-        nc.scalar.dma_start(wfx_sb[:], wf_x)
+        uiou_sb = held.tile([H, 2, GATES * H], BF16, name="uiou_sb")
         ioux_sb = held.tile([H, GATES, N], F32, name="ioux_sb")
-        nc.gpsimd.dma_start(ioux_sb[:], iou_x.rearrange("(g c) j -> c g j", g=GATES))
         c_all = held.tile([H, KN], F32, name="c_all")
-        nc.sync.dma_start(c_all[:], c_mail)
         bf_sb = held.tile([H, 1], F32, name="bf_sb")
         biou_sb = held.tile([H, GATES], F32, name="biou_sb")
-        with nc.allow_non_contiguous_dma(reason="one bias value to a partition"):
-            nc.scalar.dma_start(bf_sb[:], b_f)
-            nc.scalar.dma_start(biou_sb[:], b_iou.rearrange("(g c) o -> c (g o)", g=GATES))
         window = held.tile([H, S], F32, name="window")
-        nc.sync.dma_start(window[:], base)
+        offsets = held.tile([H, N // 16], U16, name="offsets")
 
-        h1 = held.tile([H, KN], BF16, name="h1")
-        nc.vector.tensor_tensor(h1[:], h_all[:], lab_all[:], ALU.mult)
-        h0 = held.tile([H, KN], BF16, name="h0")
-        nc.vector.tensor_tensor(h0[:], h_all[:], h1[:], ALU.subtract)
+        lab_row = lab.rearrange("o q -> (o q)")
+        for p in range(PIECES):
+            cols = slice(p * PW, (p + 1) * PW)
+            nc.sync.dma_start(lab_all[p][:], lab_row[cols].partition_broadcast(H))
+            nc.sync.dma_start(h_all[p][:], h_mail[:, cols])
+            if p == 0:
+                nc.sync.dma_start(uf_sb[:], u_f.rearrange("(s d) c -> d s c", s=2))
+        nc.sync.dma_start(wfx_sb[:], wf_x)
+        with nc.allow_non_contiguous_dma(reason="one bias value to a partition"):
+            nc.sync.dma_start(bf_sb[:], b_f)
+        nc.sync.dma_start(uiou_sb[:], u_iou.rearrange("(s d) r -> d s r", s=2))
+        nc.sync.dma_start(c_all[:], c_mail)
+        nc.sync.dma_start(ioux_sb[:], iou_x.rearrange("(g c) j -> c g j", g=GATES))
+        with nc.allow_non_contiguous_dma(reason="one bias value to a partition"):
+            nc.sync.dma_start(biou_sb[:], b_iou.rearrange("(g c) o -> c (g o)", g=GATES))
+        nc.sync.dma_start(window[:], base)
+        nc.sync.dma_start(offsets[:], offs)
+
+        zeros = held.tile([H, KN], BF16, name="zeros")
+        nc.vector.memset(zeros[:], 0.0)
+        table_warmer = held.tile([H, 1], F32, name="table_warmer")
+        nc.scalar.activation(table_warmer[:], zeros[:, 0:1], ACT.Sigmoid)
+        warm_ps = psum.tile([H, KN], F32, name="warm_ps")
+        for w in range(WARM_MATMULS):
+            nc.tensor.matmul(warm_ps[:], zeros[:, 0:H], zeros[:], start=True, stop=True)
+
+        h1 = [held.tile([H, PW], BF16, name=f"h1_{p}") for p in range(PIECES)]
+        h0 = [held.tile([H, PW], BF16, name=f"h0_{p}") for p in range(PIECES)]
+        for p in range(PIECES):
+            nc.vector.tensor_tensor(h1[p][:], h_all[p][:], lab_all[p][:], ALU.mult)
+            nc.vector.tensor_tensor(h0[p][:], h_all[p][:], h1[p][:], ALU.subtract)
         halves = (h0, h1)
 
-        f_ps = psum.tile([H, KN], F32, name="f_ps")
-        for s in range(2):
-            nc.tensor.matmul(f_ps[:], uf_sb[:, s, :], halves[s][:], start=(s == 0), stop=(s == 1))
-        f_pre = held.tile([H, K, N], F32, name="f_pre")
-        nc.vector.tensor_tensor(
-            f_pre[:],
-            f_ps[:].rearrange("c (k j) -> c k j", k=K),
-            wfx_sb[:].unsqueeze(1).to_broadcast([H, K, N]),
-            ALU.add,
-        )
-        f_gate = held.tile([H, KN], F32, name="f_gate")
-        nc.scalar.activation(
-            f_gate[:], f_pre[:].rearrange("c k j -> c (k j)"), ACT.Sigmoid, bias=bf_sb[:, 0:1]
-        )
+        f_ps = [psum.tile([H, PW], F32, name=f"f_ps{p}") for p in range(PIECES)]
+        for p in range(PIECES):
+            for s in (1, 0):
+                nc.tensor.matmul(
+                    f_ps[p][:], uf_sb[:, s, :], halves[s][p][:], start=(s == 1), stop=(s == 0)
+                )
+        f_gate = []
+        for p in range(PIECES):
+            f_pre = held.tile([H, PK, N], F32, name=f"f_pre{p}")
+            nc.vector.tensor_tensor(
+                f_pre[:],
+                f_ps[p][:].rearrange("c (k j) -> c k j", k=PK),
+                wfx_sb[:].unsqueeze(1).to_broadcast([H, PK, N]),
+                ALU.add,
+            )
+            gate = held.tile([H, PW], F32, name=f"f_gate{p}")
+            nc.scalar.activation(
+                gate[:], f_pre[:].rearrange("c k j -> c (k j)"), ACT.Sigmoid, bias=bf_sb[:, 0:1]
+            )
+            f_gate.append(gate)
 
-        functions = (ACT.Sigmoid, ACT.Sigmoid, ACT.Tanh)
-        gates = []
-        for g in range(GATES):
+        functions = {GATE_I: ACT.Sigmoid, GATE_O: ACT.Sigmoid, GATE_U: ACT.Tanh}
+        gates = {}
+        for g in (GATE_I, GATE_U, GATE_O):
             iou_ps = psum.tile([H, N], F32, name=f"iou_ps{g}")
-            for s in range(2):
+            for s in (1, 0):
                 for k in range(K):
                     nc.tensor.matmul(
                         iou_ps[:],
                         uiou_sb[:, s, g * H : (g + 1) * H],
-                        halves[s][:, k * N : (k + 1) * N],
-                        start=(s == 0 and k == 0),
-                        stop=(s == 1 and k == K - 1),
+                        halves[s][k // PK][:, (k % PK) * N : (k % PK + 1) * N],
+                        start=(s == 1 and k == 0),
+                        stop=(s == 0 and k == K - 1),
                     )
             iou_pre = held.tile([H, N], F32, name=f"iou_pre{g}")
             nc.vector.tensor_tensor(iou_pre[:], iou_ps[:], ioux_sb[:, g, :], ALU.add)
-            gate = held.tile([H, N], F32, name=f"gate{g}")
-            nc.scalar.activation(gate[:], iou_pre[:], functions[g], bias=biou_sb[:, g : g + 1])
-            gates.append(gate)
-        vi, vo, vu = gates
+            gates[g] = held.tile([H, N], F32, name=f"gate{g}")
+            nc.scalar.activation(gates[g][:], iou_pre[:], functions[g], bias=biou_sb[:, g : g + 1])
 
-        fc = held.tile([H, KN], F32, name="fc")
-        nc.vector.tensor_tensor(fc[:], f_gate[:], c_all[:], ALU.mult)
-        fc_pairs = held.tile([H, 2 * N], F32, name="fc_pairs")
-        nc.vector.tensor_tensor(fc_pairs[:], fc[:, 0 : 2 * N], fc[:, 2 * N : 4 * N], ALU.add)
-        c_agg = held.tile([H, N], F32, name="c_agg")
-        nc.vector.tensor_tensor(c_agg[:], fc_pairs[:, 0:N], fc_pairs[:, N : 2 * N], ALU.add)
+        fc_sum = []
+        for p in range(PIECES):
+            fc = held.tile([H, PW], F32, name=f"fc{p}")
+            nc.vector.tensor_tensor(fc[:], f_gate[p][:], c_all[:, p * PW : (p + 1) * PW], ALU.mult)
+            both = held.tile([H, N], F32, name=f"fc_sum{p}")
+            nc.vector.tensor_tensor(both[:], fc[:, 0:N], fc[:, N : 2 * N], ALU.add)
+            fc_sum.append(both)
         iu = held.tile([H, N], F32, name="iu")
-        nc.vector.tensor_tensor(iu[:], vi[:], vu[:], ALU.mult)
+        nc.vector.tensor_tensor(iu[:], gates[GATE_I][:], gates[GATE_U][:], ALU.mult)
+        partial = held.tile([H, N], F32, name="partial")
+        nc.vector.tensor_tensor(partial[:], fc_sum[0][:], fc_sum[1][:], ALU.add)
         cell = held.tile([H, N], F32, name="cell")
-        nc.vector.tensor_tensor(cell[:], iu[:], c_agg[:], ALU.add)
+        nc.vector.tensor_tensor(cell[:], partial[:], iu[:], ALU.add)
         tanh_cell = held.tile([H, N], F32, name="tanh_cell")
         nc.scalar.activation(tanh_cell[:], cell[:], ACT.Tanh)
 
-        nc.vector.tensor_tensor(window[:].indirect(offsets[:]), vo[:], tanh_cell[:], ALU.mult)
+        nc.vector.tensor_tensor(
+            window[:].indirect(offsets[:]), gates[GATE_O][:], tanh_cell[:], ALU.mult
+        )
         nc.sync.dma_start(out, window[:])

@@ -9,16 +9,12 @@ ACT = mybir.ActivationFunctionType
 H = 128
 K = 4
 N = 128
-KN = K * N
 S = 256
 GATE_I, GATE_O, GATE_U = 0, 1, 2
 GATES = 3
-PIECES = 2
-PK = K // PIECES
-PW = PK * N
-WARM_MATMULS = 3
+WARM_MATMULS = 4
 
-FLOPS = 2 * (2 * H) * H * KN + 2 * (2 * H) * (GATES * H) * N
+FLOPS = 2 * (2 * H) * H * (K * N) + 2 * (2 * H) * (GATES * H) * N
 
 
 def tile_improvedgraphlstmcell_kernel(
@@ -29,103 +25,92 @@ def tile_improvedgraphlstmcell_kernel(
         tc.tile_pool(name="held", bufs=1) as held,
         tc.psum_pool(name="psum", bufs=1) as psum,
     ):
-        lab_all = [held.tile([H, PW], F32, name=f"lab_all{p}") for p in range(PIECES)]
-        h_all = [held.tile([H, PW], BF16, name=f"h_all{p}") for p in range(PIECES)]
+        lab_all = held.tile([H, K * N], F32, name="lab_all")
+        h_all = held.tile([H, K * N], BF16, name="h_all")
         uf_sb = held.tile([H, 2, H], BF16, name="uf_sb")
         wfx_sb = held.tile([H, N], F32, name="wfx_sb")
         uiou_sb = held.tile([H, 2, GATES * H], BF16, name="uiou_sb")
         ioux_sb = held.tile([H, GATES, N], F32, name="ioux_sb")
-        c_all = held.tile([H, KN], F32, name="c_all")
+        c_all = held.tile([H, K * N], F32, name="c_all")
         bf_sb = held.tile([H, 1], F32, name="bf_sb")
         biou_sb = held.tile([H, GATES], F32, name="biou_sb")
         window = held.tile([H, S], F32, name="window")
         offsets = held.tile([H, N // 16], U16, name="offsets")
 
-        lab_row = lab.rearrange("o q -> (o q)")
-        for p in range(PIECES):
-            cols = slice(p * PW, (p + 1) * PW)
-            nc.sync.dma_start(lab_all[p][:], lab_row[cols].partition_broadcast(H))
-            nc.sync.dma_start(h_all[p][:], h_mail[:, cols])
-            if p == 0:
-                nc.sync.dma_start(uf_sb[:], u_f.rearrange("(s d) c -> d s c", s=2))
+        nc.sync.dma_start(lab_all[:], lab.rearrange("o q -> (o q)").partition_broadcast(H))
+        nc.scalar.dma_start(h_all[:], h_mail)
+        nc.sync.dma_start(uf_sb[:], u_f.rearrange("(s d) c -> d s c", s=2))
+        nc.scalar.dma_start(uiou_sb[:], u_iou.rearrange("(s d) r -> d s r", s=2))
+        with nc.allow_non_contiguous_dma(reason="one bias value to a partition"):
+            nc.scalar.dma_start(bf_sb[:], b_f)
+            nc.gpsimd.dma_start(biou_sb[:], b_iou.rearrange("(g c) o -> c (g o)", g=GATES))
         nc.sync.dma_start(wfx_sb[:], wf_x)
-        with nc.allow_non_contiguous_dma(reason="one bias value to a partition"):
-            nc.sync.dma_start(bf_sb[:], b_f)
-        nc.sync.dma_start(uiou_sb[:], u_iou.rearrange("(s d) r -> d s r", s=2))
         nc.sync.dma_start(c_all[:], c_mail)
-        nc.sync.dma_start(ioux_sb[:], iou_x.rearrange("(g c) j -> c g j", g=GATES))
-        with nc.allow_non_contiguous_dma(reason="one bias value to a partition"):
-            nc.sync.dma_start(biou_sb[:], b_iou.rearrange("(g c) o -> c (g o)", g=GATES))
+        nc.scalar.dma_start(ioux_sb[:], iou_x.rearrange("(g c) j -> c g j", g=GATES))
         nc.sync.dma_start(window[:], base)
         nc.sync.dma_start(offsets[:], offs)
 
-        zeros = held.tile([H, KN], BF16, name="zeros")
+        zeros = held.tile([H, K * N], BF16, name="zeros")
         nc.vector.memset(zeros[:], 0.0)
         table_warmer = held.tile([H, 1], F32, name="table_warmer")
         nc.scalar.activation(table_warmer[:], zeros[:, 0:1], ACT.Sigmoid)
-        warm_ps = psum.tile([H, KN], F32, name="warm_ps")
+        warm_ps = psum.tile([H, K * N], F32, name="warm_ps")
         for w in range(WARM_MATMULS):
             nc.tensor.matmul(warm_ps[:], zeros[:, 0:H], zeros[:], start=True, stop=True)
 
-        h1 = [held.tile([H, PW], BF16, name=f"h1_{p}") for p in range(PIECES)]
-        h0 = [held.tile([H, PW], BF16, name=f"h0_{p}") for p in range(PIECES)]
-        for p in range(PIECES):
-            nc.vector.tensor_tensor(h1[p][:], h_all[p][:], lab_all[p][:], ALU.mult)
-            nc.vector.tensor_tensor(h0[p][:], h_all[p][:], h1[p][:], ALU.subtract)
+        h0 = [held.tile([H, N], BF16, name=f"h0_{k}") for k in range(K)]
+        h1 = [held.tile([H, N], BF16, name=f"h1_{k}") for k in range(K)]
+        for k in range(K):
+            cols = slice(k * N, (k + 1) * N)
+            nc.vector.tensor_tensor(h1[k][:], h_all[:, cols], lab_all[:, cols], ALU.mult)
+            nc.vector.tensor_tensor(h0[k][:], h_all[:, cols], h1[k][:], ALU.subtract)
         halves = (h0, h1)
 
-        f_ps = [psum.tile([H, PW], F32, name=f"f_ps{p}") for p in range(PIECES)]
-        for p in range(PIECES):
+        f_ps = [psum.tile([H, N], F32, name=f"f_ps{k}") for k in range(K)]
+        for k in range(K):
             for s in (1, 0):
                 nc.tensor.matmul(
-                    f_ps[p][:], uf_sb[:, s, :], halves[s][p][:], start=(s == 1), stop=(s == 0)
+                    f_ps[k][:], uf_sb[:, s, :], halves[s][k][:], start=(s == 1), stop=(s == 0)
                 )
-        f_gate = []
-        for p in range(PIECES):
-            f_pre = held.tile([H, PK, N], F32, name=f"f_pre{p}")
-            nc.vector.tensor_tensor(
-                f_pre[:],
-                f_ps[p][:].rearrange("c (k j) -> c k j", k=PK),
-                wfx_sb[:].unsqueeze(1).to_broadcast([H, PK, N]),
-                ALU.add,
-            )
-            gate = held.tile([H, PW], F32, name=f"f_gate{p}")
-            nc.scalar.activation(
-                gate[:], f_pre[:].rearrange("c k j -> c (k j)"), ACT.Sigmoid, bias=bf_sb[:, 0:1]
-            )
-            f_gate.append(gate)
+        iou_ps = [psum.tile([H, N], F32, name=f"iou_ps{g}") for g in range(GATES)]
+        for g in (GATE_I, GATE_U, GATE_O):
+            for k in range(K):
+                for s in (1, 0):
+                    nc.tensor.matmul(
+                        iou_ps[g][:],
+                        uiou_sb[:, s, g * H : (g + 1) * H],
+                        halves[s][k][:],
+                        start=(k == 0 and s == 1),
+                        stop=(k == K - 1 and s == 0),
+                    )
+
+        c_agg = None
+        for k in range(K):
+            f_pre = held.tile([H, N], F32, name=f"f_pre{k}")
+            nc.vector.tensor_tensor(f_pre[:], f_ps[k][:], wfx_sb[:], ALU.add)
+            f_gate = held.tile([H, N], F32, name=f"f_gate{k}")
+            nc.scalar.activation(f_gate[:], f_pre[:], ACT.Sigmoid, bias=bf_sb[:, 0:1])
+            fc = held.tile([H, N], F32, name=f"fc{k}")
+            nc.vector.tensor_tensor(fc[:], f_gate[:], c_all[:, k * N : (k + 1) * N], ALU.mult)
+            if k == 0:
+                c_agg = fc
+            else:
+                longer = held.tile([H, N], F32, name=f"c_agg{k}")
+                nc.vector.tensor_tensor(longer[:], c_agg[:], fc[:], ALU.add)
+                c_agg = longer
 
         functions = {GATE_I: ACT.Sigmoid, GATE_O: ACT.Sigmoid, GATE_U: ACT.Tanh}
         gates = {}
         for g in (GATE_I, GATE_U, GATE_O):
-            iou_ps = psum.tile([H, N], F32, name=f"iou_ps{g}")
-            for s in (1, 0):
-                for k in range(K):
-                    nc.tensor.matmul(
-                        iou_ps[:],
-                        uiou_sb[:, s, g * H : (g + 1) * H],
-                        halves[s][k // PK][:, (k % PK) * N : (k % PK + 1) * N],
-                        start=(s == 1 and k == 0),
-                        stop=(s == 0 and k == K - 1),
-                    )
             iou_pre = held.tile([H, N], F32, name=f"iou_pre{g}")
-            nc.vector.tensor_tensor(iou_pre[:], iou_ps[:], ioux_sb[:, g, :], ALU.add)
+            nc.vector.tensor_tensor(iou_pre[:], iou_ps[g][:], ioux_sb[:, g, :], ALU.add)
             gates[g] = held.tile([H, N], F32, name=f"gate{g}")
             nc.scalar.activation(gates[g][:], iou_pre[:], functions[g], bias=biou_sb[:, g : g + 1])
 
-        fc_sum = []
-        for p in range(PIECES):
-            fc = held.tile([H, PW], F32, name=f"fc{p}")
-            nc.vector.tensor_tensor(fc[:], f_gate[p][:], c_all[:, p * PW : (p + 1) * PW], ALU.mult)
-            both = held.tile([H, N], F32, name=f"fc_sum{p}")
-            nc.vector.tensor_tensor(both[:], fc[:, 0:N], fc[:, N : 2 * N], ALU.add)
-            fc_sum.append(both)
         iu = held.tile([H, N], F32, name="iu")
         nc.vector.tensor_tensor(iu[:], gates[GATE_I][:], gates[GATE_U][:], ALU.mult)
-        partial = held.tile([H, N], F32, name="partial")
-        nc.vector.tensor_tensor(partial[:], fc_sum[0][:], fc_sum[1][:], ALU.add)
         cell = held.tile([H, N], F32, name="cell")
-        nc.vector.tensor_tensor(cell[:], partial[:], iu[:], ALU.add)
+        nc.vector.tensor_tensor(cell[:], c_agg[:], iu[:], ALU.add)
         tanh_cell = held.tile([H, N], F32, name="tanh_cell")
         nc.scalar.activation(tanh_cell[:], cell[:], ACT.Tanh)
 

@@ -12,7 +12,7 @@ N = 128
 S = 256
 GATE_I, GATE_O, GATE_U = 0, 1, 2
 GATES = 3
-WARM_MATMULS = 4
+WARM_MATMULS = 3
 
 FLOPS = 2 * (2 * H) * H * (K * N) + 2 * (2 * H) * (GATES * H) * N
 
@@ -43,10 +43,11 @@ def tile_improvedgraphlstmcell_kernel(
         nc.scalar.dma_start(uiou_sb[:], u_iou.rearrange("(s d) r -> d s r", s=2))
         with nc.allow_non_contiguous_dma(reason="one bias value to a partition"):
             nc.scalar.dma_start(bf_sb[:], b_f)
-            nc.gpsimd.dma_start(biou_sb[:], b_iou.rearrange("(g c) o -> c (g o)", g=GATES))
         nc.sync.dma_start(wfx_sb[:], wf_x)
         nc.sync.dma_start(c_all[:], c_mail)
         nc.scalar.dma_start(ioux_sb[:], iou_x.rearrange("(g c) j -> c g j", g=GATES))
+        with nc.allow_non_contiguous_dma(reason="one bias value to a partition"):
+            nc.sync.dma_start(biou_sb[:], b_iou.rearrange("(g c) o -> c (g o)", g=GATES))
         nc.sync.dma_start(window[:], base)
         nc.sync.dma_start(offsets[:], offs)
 

@@ -12,7 +12,6 @@ N = 128
 S = 256
 GATE_I, GATE_O, GATE_U = 0, 1, 2
 GATES = 3
-WARM_MATMULS = 3
 
 FLOPS = 2 * (2 * H) * H * (K * N) + 2 * (2 * H) * (GATES * H) * N
 
@@ -51,13 +50,10 @@ def tile_improvedgraphlstmcell_kernel(
         nc.sync.dma_start(window[:], base)
         nc.sync.dma_start(offsets[:], offs)
 
-        zeros = held.tile([H, K * N], BF16, name="zeros")
+        zeros = held.tile([H, 1], F32, name="zeros")
         nc.vector.memset(zeros[:], 0.0)
         table_warmer = held.tile([H, 1], F32, name="table_warmer")
-        nc.scalar.activation(table_warmer[:], zeros[:, 0:1], ACT.Sigmoid)
-        warm_ps = psum.tile([H, K * N], F32, name="warm_ps")
-        for w in range(WARM_MATMULS):
-            nc.tensor.matmul(warm_ps[:], zeros[:, 0:H], zeros[:], start=True, stop=True)
+        nc.scalar.activation(table_warmer[:], zeros[:], ACT.Sigmoid)
 
         h0 = [held.tile([H, N], BF16, name=f"h0_{k}") for k in range(K)]
         h1 = [held.tile([H, N], BF16, name=f"h1_{k}") for k in range(K)]

@@ -36,17 +36,16 @@ def tile_improvedgraphlstmcell_kernel(
         window = held.tile([H, S], F32, name="window")
         offsets = held.tile([H, N // 16], U16, name="offsets")
 
+        nc.sync.dma_start(uf_sb[:], u_f.rearrange("(s d) c -> d s c", s=2))
         nc.sync.dma_start(lab_all[:], lab.rearrange("o q -> (o q)").partition_broadcast(H))
         nc.scalar.dma_start(h_all[:], h_mail)
-        nc.sync.dma_start(uf_sb[:], u_f.rearrange("(s d) c -> d s c", s=2))
         nc.scalar.dma_start(uiou_sb[:], u_iou.rearrange("(s d) r -> d s r", s=2))
         with nc.allow_non_contiguous_dma(reason="one bias value to a partition"):
             nc.scalar.dma_start(bf_sb[:], b_f)
+            nc.scalar.dma_start(biou_sb[:], b_iou.rearrange("(g c) o -> c (g o)", g=GATES))
         nc.sync.dma_start(wfx_sb[:], wf_x)
         nc.sync.dma_start(c_all[:], c_mail)
-        nc.scalar.dma_start(ioux_sb[:], iou_x.rearrange("(g c) j -> c g j", g=GATES))
-        with nc.allow_non_contiguous_dma(reason="one bias value to a partition"):
-            nc.sync.dma_start(biou_sb[:], b_iou.rearrange("(g c) o -> c (g o)", g=GATES))
+        nc.sync.dma_start(ioux_sb[:], iou_x.rearrange("(g c) j -> c g j", g=GATES))
         nc.sync.dma_start(window[:], base)
         nc.sync.dma_start(offsets[:], offs)
 

@@ -12,6 +12,7 @@ N = 128
 S = 256
 GATE_I, GATE_O, GATE_U = 0, 1, 2
 GATES = 3
+WARM_MATMULS = 3
 
 FLOPS = 2 * (2 * H) * H * (K * N) + 2 * (2 * H) * (GATES * H) * N
 
@@ -42,17 +43,21 @@ def tile_improvedgraphlstmcell_kernel(
         nc.scalar.dma_start(uiou_sb[:], u_iou.rearrange("(s d) r -> d s r", s=2))
         with nc.allow_non_contiguous_dma(reason="one bias value to a partition"):
             nc.scalar.dma_start(bf_sb[:], b_f)
-            nc.scalar.dma_start(biou_sb[:], b_iou.rearrange("(g c) o -> c (g o)", g=GATES))
         nc.sync.dma_start(wfx_sb[:], wf_x)
         nc.sync.dma_start(c_all[:], c_mail)
-        nc.sync.dma_start(ioux_sb[:], iou_x.rearrange("(g c) j -> c g j", g=GATES))
+        nc.scalar.dma_start(ioux_sb[:], iou_x.rearrange("(g c) j -> c g j", g=GATES))
+        with nc.allow_non_contiguous_dma(reason="one bias value to a partition"):
+            nc.sync.dma_start(biou_sb[:], b_iou.rearrange("(g c) o -> c (g o)", g=GATES))
         nc.sync.dma_start(window[:], base)
         nc.sync.dma_start(offsets[:], offs)
 
-        zeros = held.tile([H, 1], F32, name="zeros")
+        zeros = held.tile([H, K * N], BF16, name="zeros")
         nc.vector.memset(zeros[:], 0.0)
         table_warmer = held.tile([H, 1], F32, name="table_warmer")
-        nc.scalar.activation(table_warmer[:], zeros[:], ACT.Sigmoid)
+        nc.scalar.activation(table_warmer[:], zeros[:, 0:1], ACT.Sigmoid)
+        warm_ps = psum.tile([H, K * N], F32, name="warm_ps")
+        for w in range(WARM_MATMULS):
+            nc.tensor.matmul(warm_ps[:], zeros[:, 0:H], zeros[:], start=True, stop=True)
 
         h0 = [held.tile([H, N], BF16, name=f"h0_{k}") for k in range(K)]
         h1 = [held.tile([H, N], BF16, name=f"h1_{k}") for k in range(K)]

@@ -12,7 +12,6 @@ N = 128
 S = 256
 GATE_I, GATE_O, GATE_U = 0, 1, 2
 GATES = 3
-WARM_MATMULS = 3
 
 FLOPS = 2 * (2 * H) * H * (K * N) + 2 * (2 * H) * (GATES * H) * N
 
@@ -37,9 +36,9 @@ def tile_improvedgraphlstmcell_kernel(
         window = held.tile([H, S], F32, name="window")
         offsets = held.tile([H, N // 16], U16, name="offsets")
 
-        nc.sync.dma_start(uf_sb[:], u_f.rearrange("(s d) c -> d s c", s=2))
         nc.sync.dma_start(lab_all[:], lab.rearrange("o q -> (o q)").partition_broadcast(H))
         nc.scalar.dma_start(h_all[:], h_mail)
+        nc.sync.dma_start(uf_sb[:], u_f.rearrange("(s d) c -> d s c", s=2))
         nc.scalar.dma_start(uiou_sb[:], u_iou.rearrange("(s d) r -> d s r", s=2))
         with nc.allow_non_contiguous_dma(reason="one bias value to a partition"):
             nc.scalar.dma_start(bf_sb[:], b_f)
@@ -51,21 +50,26 @@ def tile_improvedgraphlstmcell_kernel(
         nc.sync.dma_start(window[:], base)
         nc.sync.dma_start(offsets[:], offs)
 
-        zeros = held.tile([H, K * N], BF16, name="zeros")
+        zeros = held.tile([H, 1], F32, name="zeros")
         nc.vector.memset(zeros[:], 0.0)
         table_warmer = held.tile([H, 1], F32, name="table_warmer")
-        nc.scalar.activation(table_warmer[:], zeros[:, 0:1], ACT.Sigmoid)
-        warm_ps = psum.tile([H, K * N], F32, name="warm_ps")
-        for w in range(WARM_MATMULS):
-            nc.tensor.matmul(warm_ps[:], zeros[:, 0:H], zeros[:], start=True, stop=True)
+        nc.scalar.activation(table_warmer[:], zeros[:], ACT.Sigmoid)
 
         h0 = [held.tile([H, N], BF16, name=f"h0_{k}") for k in range(K)]
         h1 = [held.tile([H, N], BF16, name=f"h1_{k}") for k in range(K)]
+        halves = (h0, h1)
+        sums = [None, None]
         for k in range(K):
             cols = slice(k * N, (k + 1) * N)
             nc.vector.tensor_tensor(h1[k][:], h_all[:, cols], lab_all[:, cols], ALU.mult)
             nc.vector.tensor_tensor(h0[k][:], h_all[:, cols], h1[k][:], ALU.subtract)
-        halves = (h0, h1)
+            for s in (1, 0):
+                if k == 0:
+                    sums[s] = halves[s][0]
+                else:
+                    longer = held.tile([H, N], BF16 if k == K - 1 else F32, name=f"sum{s}_{k}")
+                    nc.vector.tensor_tensor(longer[:], sums[s][:], halves[s][k][:], ALU.add)
+                    sums[s] = longer
 
         f_ps = [psum.tile([H, N], F32, name=f"f_ps{k}") for k in range(K)]
         for k in range(K):
@@ -75,15 +79,14 @@ def tile_improvedgraphlstmcell_kernel(
                 )
         iou_ps = [psum.tile([H, N], F32, name=f"iou_ps{g}") for g in range(GATES)]
         for g in (GATE_I, GATE_U, GATE_O):
-            for k in range(K):
-                for s in (1, 0):
-                    nc.tensor.matmul(
-                        iou_ps[g][:],
-                        uiou_sb[:, s, g * H : (g + 1) * H],
-                        halves[s][k][:],
-                        start=(k == 0 and s == 1),
-                        stop=(k == K - 1 and s == 0),
-                    )
+            for s in (1, 0):
+                nc.tensor.matmul(
+                    iou_ps[g][:],
+                    uiou_sb[:, s, g * H : (g + 1) * H],
+                    sums[s][:],
+                    start=(s == 1),
+                    stop=(s == 0),
+                )
 
         c_agg = None
         for k in range(K):

@@ -36,15 +36,15 @@ def tile_improvedgraphlstmcell_kernel(
         window = held.tile([H, S], F32, name="window")
         offsets = held.tile([H, N // 16], U16, name="offsets")
 
-        nc.sync.dma_start(lab_all[:], lab.rearrange("o q -> (o q)").partition_broadcast(H))
         nc.scalar.dma_start(h_all[:], h_mail)
+        nc.sync.dma_start(lab_all[:], lab.rearrange("o q -> (o q)").partition_broadcast(H))
         nc.sync.dma_start(uf_sb[:], u_f.rearrange("(s d) c -> d s c", s=2))
-        nc.scalar.dma_start(uiou_sb[:], u_iou.rearrange("(s d) r -> d s r", s=2))
         with nc.allow_non_contiguous_dma(reason="one bias value to a partition"):
             nc.scalar.dma_start(bf_sb[:], b_f)
         nc.sync.dma_start(wfx_sb[:], wf_x)
+        nc.sync.dma_start(uiou_sb[:], u_iou.rearrange("(s d) r -> d s r", s=2))
         nc.sync.dma_start(c_all[:], c_mail)
-        nc.scalar.dma_start(ioux_sb[:], iou_x.rearrange("(g c) j -> c g j", g=GATES))
+        nc.sync.dma_start(ioux_sb[:], iou_x.rearrange("(g c) j -> c g j", g=GATES))
         with nc.allow_non_contiguous_dma(reason="one bias value to a partition"):
             nc.sync.dma_start(biou_sb[:], b_iou.rearrange("(g c) o -> c (g o)", g=GATES))
         nc.sync.dma_start(window[:], base)

@@ -12,6 +12,7 @@ N = 128
 S = 256
 GATE_I, GATE_O, GATE_U = 0, 1, 2
 GATES = 3
+ROWS = 32
 
 FLOPS = 2 * (2 * H) * H * (K * N) + 2 * (2 * H) * (GATES * H) * N
 
@@ -24,7 +25,7 @@ def tile_improvedgraphlstmcell_kernel(
         tc.tile_pool(name="held", bufs=1) as held,
         tc.psum_pool(name="psum", bufs=1) as psum,
     ):
-        lab_all = held.tile([H, K * N], F32, name="lab_all")
+        lab_rows = held.tile([ROWS, K * N, 2], BF16, name="lab_rows")
         h_all = held.tile([H, K * N], BF16, name="h_all")
         uf_sb = held.tile([H, 2, H], BF16, name="uf_sb")
         wfx_sb = held.tile([H, N], F32, name="wfx_sb")
@@ -37,7 +38,10 @@ def tile_improvedgraphlstmcell_kernel(
         offsets = held.tile([H, N // 16], U16, name="offsets")
 
         nc.scalar.dma_start(h_all[:], h_mail)
-        nc.sync.dma_start(lab_all[:], lab.rearrange("o q -> (o q)").partition_broadcast(H))
+        nc.sync.dma_start(
+            lab_rows[:].rearrange("p q t -> p (q t)"),
+            lab.bitcast(BF16).rearrange("o q -> (o q)").partition_broadcast(ROWS),
+        )
         nc.sync.dma_start(uf_sb[:], u_f.rearrange("(s d) c -> d s c", s=2))
         with nc.allow_non_contiguous_dma(reason="one bias value to a partition"):
             nc.scalar.dma_start(bf_sb[:], b_f)
@@ -54,14 +58,21 @@ def tile_improvedgraphlstmcell_kernel(
         nc.vector.memset(zeros[:], 0.0)
         table_warmer = held.tile([H, 1], F32, name="table_warmer")
         nc.scalar.activation(table_warmer[:], zeros[:], ACT.Sigmoid)
+        mean_rows = held.tile([ROWS, H], BF16, name="mean_rows")
+        nc.vector.memset(mean_rows[:], 1.0 / ROWS)
 
         h0 = [held.tile([H, N], BF16, name=f"h0_{k}") for k in range(K)]
         h1 = [held.tile([H, N], BF16, name=f"h1_{k}") for k in range(K)]
         halves = (h0, h1)
         sums = [None, None]
+        lab_ps = [psum.tile([H, N], F32, name=f"lab_ps{k}", tag=f"neighbour{k}") for k in range(K)]
+        for k in range(K):
+            nc.tensor.matmul(
+                lab_ps[k][:], mean_rows[:], lab_rows[:, k * N : (k + 1) * N, 1], start=True, stop=True
+            )
         for k in range(K):
             cols = slice(k * N, (k + 1) * N)
-            nc.vector.tensor_tensor(h1[k][:], h_all[:, cols], lab_all[:, cols], ALU.mult)
+            nc.vector.tensor_tensor(h1[k][:], h_all[:, cols], lab_ps[k][:], ALU.mult)
             nc.vector.tensor_tensor(h0[k][:], h_all[:, cols], h1[k][:], ALU.subtract)
             for s in (1, 0):
                 if k == 0:
@@ -71,7 +82,7 @@ def tile_improvedgraphlstmcell_kernel(
                     nc.vector.tensor_tensor(longer[:], sums[s][:], halves[s][k][:], ALU.add)
                     sums[s] = longer
 
-        f_ps = [psum.tile([H, N], F32, name=f"f_ps{k}") for k in range(K)]
+        f_ps = [psum.tile([H, N], F32, name=f"f_ps{k}", tag=f"neighbour{k}") for k in range(K)]
         for k in range(K):
             for s in (1, 0):
                 nc.tensor.matmul(

@@ -25,7 +25,7 @@ def tile_improvedgraphlstmcell_kernel(
         tc.tile_pool(name="held", bufs=1) as held,
         tc.psum_pool(name="psum", bufs=1) as psum,
     ):
-        lab_rows = held.tile([ROWS, K * N, 2], BF16, name="lab_rows")
+        lab_rows = held.tile([ROWS, 2 * K * N], BF16, name="lab_rows")
         h_all = held.tile([H, K * N], BF16, name="h_all")
         uf_sb = held.tile([H, 2, H], BF16, name="uf_sb")
         wfx_sb = held.tile([H, N], F32, name="wfx_sb")
@@ -38,10 +38,8 @@ def tile_improvedgraphlstmcell_kernel(
         offsets = held.tile([H, N // 16], U16, name="offsets")
 
         nc.scalar.dma_start(h_all[:], h_mail)
-        nc.sync.dma_start(
-            lab_rows[:].rearrange("p q t -> p (q t)"),
-            lab.bitcast(BF16).rearrange("o q -> (o q)").partition_broadcast(ROWS),
-        )
+        nc.gpsimd.memset(lab_rows[:].bitcast(F32), 0.0)
+        nc.sync.dma_start(lab_rows[0:1, :], lab.bitcast(BF16))
         nc.sync.dma_start(uf_sb[:], u_f.rearrange("(s d) c -> d s c", s=2))
         with nc.allow_non_contiguous_dma(reason="one bias value to a partition"):
             nc.scalar.dma_start(bf_sb[:], b_f)
@@ -58,8 +56,8 @@ def tile_improvedgraphlstmcell_kernel(
         nc.vector.memset(zeros[:], 0.0)
         table_warmer = held.tile([H, 1], F32, name="table_warmer")
         nc.scalar.activation(table_warmer[:], zeros[:], ACT.Sigmoid)
-        mean_rows = held.tile([ROWS, H], BF16, name="mean_rows")
-        nc.vector.memset(mean_rows[:], 1.0 / ROWS)
+        ones = held.tile([ROWS, H], BF16, name="ones")
+        nc.vector.memset(ones[:], 1.0)
 
         h0 = [held.tile([H, N], BF16, name=f"h0_{k}") for k in range(K)]
         h1 = [held.tile([H, N], BF16, name=f"h1_{k}") for k in range(K)]
@@ -68,7 +66,7 @@ def tile_improvedgraphlstmcell_kernel(
         lab_ps = [psum.tile([H, N], F32, name=f"lab_ps{k}", tag=f"neighbour{k}") for k in range(K)]
         for k in range(K):
             nc.tensor.matmul(
-                lab_ps[k][:], mean_rows[:], lab_rows[:, k * N : (k + 1) * N, 1], start=True, stop=True
+                lab_ps[k][:], ones[:], lab_rows[:, 2 * k * N + 1 : 2 * (k + 1) * N : 2], start=True, stop=True
             )
         for k in range(K):
             cols = slice(k * N, (k + 1) * N)

@@ -38,8 +38,8 @@ def tile_improvedgraphlstmcell_kernel(
         offsets = held.tile([H, N // 16], U16, name="offsets")
 
         nc.scalar.dma_start(h_all[:], h_mail)
-        nc.gpsimd.memset(lab_rows[:].bitcast(F32), 0.0)
-        nc.sync.dma_start(lab_rows[0:1, :], lab.bitcast(BF16))
+        nc.sync.dma_start(lab_rows[ROWS - 1 : ROWS, :], lab.bitcast(BF16))
+        nc.gpsimd.memset(lab_rows[0 : ROWS - 1, :].bitcast(F32), 0.0)
         nc.sync.dma_start(uf_sb[:], u_f.rearrange("(s d) c -> d s c", s=2))
         with nc.allow_non_contiguous_dma(reason="one bias value to a partition"):
             nc.scalar.dma_start(bf_sb[:], b_f)

@@ -12,7 +12,8 @@ N = 128
 S = 256
 GATE_I, GATE_O, GATE_U = 0, 1, 2
 GATES = 3
-ROWS = 32
+PAIRS = 2
+BANK = 512
 
 FLOPS = 2 * (2 * H) * H * (K * N) + 2 * (2 * H) * (GATES * H) * N
 
@@ -25,7 +26,7 @@ def tile_improvedgraphlstmcell_kernel(
         tc.tile_pool(name="held", bufs=1) as held,
         tc.psum_pool(name="psum", bufs=1) as psum,
     ):
-        lab_rows = held.tile([ROWS, 2 * K * N], BF16, name="lab_rows")
+        lab_rows = held.tile([H, 2 * K * N], BF16, name="lab_rows")
         h_all = held.tile([H, K * N], BF16, name="h_all")
         uf_sb = held.tile([H, 2, H], BF16, name="uf_sb")
         wfx_sb = held.tile([H, N], F32, name="wfx_sb")
@@ -38,8 +39,8 @@ def tile_improvedgraphlstmcell_kernel(
         offsets = held.tile([H, N // 16], U16, name="offsets")
 
         nc.scalar.dma_start(h_all[:], h_mail)
-        nc.sync.dma_start(lab_rows[ROWS - 1 : ROWS, :], lab.bitcast(BF16))
-        nc.gpsimd.memset(lab_rows[0 : ROWS - 1, :].bitcast(F32), 0.0)
+        nc.sync.dma_start(lab_rows[H - 1 : H, :], lab.bitcast(BF16))
+        nc.gpsimd.memset(lab_rows[0 : H - 1, :].bitcast(F32), 0.0)
         nc.sync.dma_start(uf_sb[:], u_f.rearrange("(s d) c -> d s c", s=2))
         with nc.allow_non_contiguous_dma(reason="one bias value to a partition"):
             nc.scalar.dma_start(bf_sb[:], b_f)
@@ -56,14 +57,14 @@ def tile_improvedgraphlstmcell_kernel(
         nc.vector.memset(zeros[:], 0.0)
         table_warmer = held.tile([H, 1], F32, name="table_warmer")
         nc.scalar.activation(table_warmer[:], zeros[:], ACT.Sigmoid)
-        ones = held.tile([ROWS, H], BF16, name="ones")
+        ones = held.tile([H, H], BF16, name="ones")
         nc.vector.memset(ones[:], 1.0)
 
         h0 = [held.tile([H, N], BF16, name=f"h0_{k}") for k in range(K)]
         h1 = [held.tile([H, N], BF16, name=f"h1_{k}") for k in range(K)]
         halves = (h0, h1)
-        sums = [None, None]
-        lab_ps = [psum.tile([H, N], F32, name=f"lab_ps{k}", tag=f"neighbour{k}") for k in range(K)]
+        pair_sum = [[held.tile([H, N], BF16, name=f"pair_sum{s}_{p}") for p in range(PAIRS)] for s in range(2)]
+        lab_ps = [psum.tile([H, N], BF16, name=f"lab_ps{k}", tag=f"neighbour{k}") for k in range(K)]
         for k in range(K):
             nc.tensor.matmul(
                 lab_ps[k][:], ones[:], lab_rows[:, 2 * k * N + 1 : 2 * (k + 1) * N : 2], start=True, stop=True
@@ -72,13 +73,11 @@ def tile_improvedgraphlstmcell_kernel(
             cols = slice(k * N, (k + 1) * N)
             nc.vector.tensor_tensor(h1[k][:], h_all[:, cols], lab_ps[k][:], ALU.mult)
             nc.vector.tensor_tensor(h0[k][:], h_all[:, cols], h1[k][:], ALU.subtract)
-            for s in (1, 0):
-                if k == 0:
-                    sums[s] = halves[s][0]
-                else:
-                    longer = held.tile([H, N], BF16 if k == K - 1 else F32, name=f"sum{s}_{k}")
-                    nc.vector.tensor_tensor(longer[:], sums[s][:], halves[s][k][:], ALU.add)
-                    sums[s] = longer
+            if k % 2 == 1:
+                for s in (1, 0):
+                    nc.vector.tensor_tensor(
+                        pair_sum[s][k // 2][:], halves[s][k - 1][:], halves[s][k][:], ALU.add
+                    )
 
         f_ps = [psum.tile([H, N], F32, name=f"f_ps{k}", tag=f"neighbour{k}") for k in range(K)]
         for k in range(K):
@@ -86,16 +85,17 @@ def tile_improvedgraphlstmcell_kernel(
                 nc.tensor.matmul(
                     f_ps[k][:], uf_sb[:, s, :], halves[s][k][:], start=(s == 1), stop=(s == 0)
                 )
-        iou_ps = [psum.tile([H, N], F32, name=f"iou_ps{g}") for g in range(GATES)]
-        for g in (GATE_I, GATE_U, GATE_O):
-            for s in (1, 0):
-                nc.tensor.matmul(
-                    iou_ps[g][:],
-                    uiou_sb[:, s, g * H : (g + 1) * H],
-                    sums[s][:],
-                    start=(s == 1),
-                    stop=(s == 0),
-                )
+        iou_ps = [psum.tile([H, BANK], F32, name=f"iou_ps{g}") for g in range(GATES)]
+        for p in range(PAIRS):
+            for g in (GATE_I, GATE_U, GATE_O):
+                for s in (1, 0):
+                    nc.tensor.matmul(
+                        iou_ps[g][:, 0:N],
+                        uiou_sb[:, s, g * H : (g + 1) * H],
+                        pair_sum[s][p][:],
+                        start=(p == 0 and s == 1),
+                        stop=(p == PAIRS - 1 and s == 0),
+                    )
 
         c_agg = None
         for k in range(K):
@@ -116,7 +116,7 @@ def tile_improvedgraphlstmcell_kernel(
         gates = {}
         for g in (GATE_I, GATE_U, GATE_O):
             iou_pre = held.tile([H, N], F32, name=f"iou_pre{g}")
-            nc.vector.tensor_tensor(iou_pre[:], iou_ps[g][:], ioux_sb[:, g, :], ALU.add)
+            nc.vector.tensor_tensor(iou_pre[:], iou_ps[g][:, 0:N], ioux_sb[:, g, :], ALU.add)
             gates[g] = held.tile([H, N], F32, name=f"gate{g}")
             nc.scalar.activation(gates[g][:], iou_pre[:], functions[g], bias=biou_sb[:, g : g + 1])
 

@@ -85,9 +85,13 @@ def tile_improvedgraphlstmcell_kernel(
                 nc.tensor.matmul(
                     f_ps[k][:], uf_sb[:, s, :], halves[s][k][:], start=(s == 1), stop=(s == 0)
                 )
-        iou_ps = [psum.tile([H, BANK], F32, name=f"iou_ps{g}") for g in range(GATES)]
-        for p in range(PAIRS):
-            for g in (GATE_I, GATE_U, GATE_O):
+        iou_ps = {
+            GATE_I: psum.tile([H, BANK], F32, name="i_ps"),
+            GATE_U: psum.tile([H, BANK], F32, name="u_ps"),
+        }
+
+        def gate_products(g):
+            for p in range(PAIRS):
                 for s in (1, 0):
                     nc.tensor.matmul(
                         iou_ps[g][:, 0:N],
@@ -96,6 +100,9 @@ def tile_improvedgraphlstmcell_kernel(
                         start=(p == 0 and s == 1),
                         stop=(p == PAIRS - 1 and s == 0),
                     )
+
+        gate_products(GATE_I)
+        gate_products(GATE_U)
 
         c_agg = None
         for k in range(K):
@@ -111,6 +118,9 @@ def tile_improvedgraphlstmcell_kernel(
                 longer = held.tile([H, N], F32, name=f"c_agg{k}")
                 nc.vector.tensor_tensor(longer[:], c_agg[:], fc[:], ALU.add)
                 c_agg = longer
+
+        iou_ps[GATE_O] = psum.tile([H, N], F32, name="o_ps", tag=f"neighbour{K - 1}")
+        gate_products(GATE_O)
 
         functions = {GATE_I: ACT.Sigmoid, GATE_O: ACT.Sigmoid, GATE_U: ACT.Tanh}
         gates = {}

@@ -60,10 +60,8 @@ def tile_improvedgraphlstmcell_kernel(
         ones = held.tile([H, H], BF16, name="ones")
         nc.vector.memset(ones[:], 1.0)
 
-        h0 = [held.tile([H, N], BF16, name=f"h0_{k}") for k in range(K)]
-        h1 = [held.tile([H, N], BF16, name=f"h1_{k}") for k in range(K)]
-        halves = (h0, h1)
-        pair_sum = [[held.tile([H, N], BF16, name=f"pair_sum{s}_{p}") for p in range(PAIRS)] for s in range(2)]
+        routed = [held.tile([H, 2, N], BF16, name=f"routed{k}") for k in range(K)]
+        pair_sum = [held.tile([H, 2, N], BF16, name=f"pair_sum{p}") for p in range(PAIRS)]
         lab_ps = [psum.tile([H, N], BF16, name=f"lab_ps{k}", tag=f"neighbour{k}") for k in range(K)]
         for k in range(K):
             nc.tensor.matmul(
@@ -71,19 +69,17 @@ def tile_improvedgraphlstmcell_kernel(
             )
         for k in range(K):
             cols = slice(k * N, (k + 1) * N)
-            nc.vector.tensor_tensor(h1[k][:], h_all[:, cols], lab_ps[k][:], ALU.mult)
-            nc.vector.tensor_tensor(h0[k][:], h_all[:, cols], h1[k][:], ALU.subtract)
+            h0, h1 = routed[k][:, 0, :], routed[k][:, 1, :]
+            nc.vector.tensor_tensor(h1, h_all[:, cols], lab_ps[k][:], ALU.mult)
+            nc.vector.tensor_tensor(h0, h_all[:, cols], h1, ALU.subtract)
             if k % 2 == 1:
-                for s in (1, 0):
-                    nc.vector.tensor_tensor(
-                        pair_sum[s][k // 2][:], halves[s][k - 1][:], halves[s][k][:], ALU.add
-                    )
+                nc.vector.tensor_tensor(pair_sum[k // 2][:], routed[k - 1][:], routed[k][:], ALU.add)
 
         f_ps = [psum.tile([H, N], F32, name=f"f_ps{k}", tag=f"neighbour{k}") for k in range(K)]
         for k in range(K):
             for s in (1, 0):
                 nc.tensor.matmul(
-                    f_ps[k][:], uf_sb[:, s, :], halves[s][k][:], start=(s == 1), stop=(s == 0)
+                    f_ps[k][:], uf_sb[:, s, :], routed[k][:, s, :], start=(s == 1), stop=(s == 0)
                 )
         iou_ps = {
             GATE_I: psum.tile([H, BANK], F32, name="i_ps"),
@@ -96,7 +92,7 @@ def tile_improvedgraphlstmcell_kernel(
                     nc.tensor.matmul(
                         iou_ps[g][:, 0:N],
                         uiou_sb[:, s, g * H : (g + 1) * H],
-                        pair_sum[s][p][:],
+                        pair_sum[p][:, s, :],
                         start=(p == 0 and s == 1),
                         stop=(p == PAIRS - 1 and s == 0),
                     )
@@ -130,12 +126,14 @@ def tile_improvedgraphlstmcell_kernel(
             gates[g] = held.tile([H, N], F32, name=f"gate{g}")
             nc.scalar.activation(gates[g][:], iou_pre[:], functions[g], bias=biou_sb[:, g : g + 1])
 
-        iu = held.tile([H, N], F32, name="iu")
-        nc.vector.tensor_tensor(iu[:], gates[GATE_I][:], gates[GATE_U][:], ALU.mult)
-        cell = held.tile([H, N], F32, name="cell")
-        nc.vector.tensor_tensor(cell[:], c_agg[:], iu[:], ALU.add)
         tanh_cell = held.tile([H, N], F32, name="tanh_cell")
-        nc.scalar.activation(tanh_cell[:], cell[:], ACT.Tanh)
+        for half in range(2):
+            nodes = slice(half * N // 2, (half + 1) * N // 2)
+            iu = held.tile([H, N // 2], F32, name=f"iu{half}")
+            nc.vector.tensor_tensor(iu[:], gates[GATE_I][:, nodes], gates[GATE_U][:, nodes], ALU.mult)
+            cell = held.tile([H, N // 2], F32, name=f"cell{half}")
+            nc.vector.tensor_tensor(cell[:], c_agg[:, nodes], iu[:], ALU.add)
+            nc.scalar.activation(tanh_cell[:, nodes], cell[:], ACT.Tanh)
 
         nc.vector.tensor_tensor(
             window[:].indirect(offsets[:]), gates[GATE_O][:], tanh_cell[:], ALU.mult

@@ -49,7 +49,7 @@ def tile_improvedgraphlstmcell_kernel(
         nc.sync.dma_start(c_all[:], c_mail)
         nc.sync.dma_start(ioux_sb[:], iou_x.rearrange("(g c) j -> c g j", g=GATES))
         with nc.allow_non_contiguous_dma(reason="one bias value to a partition"):
-            nc.sync.dma_start(biou_sb[:], b_iou.rearrange("(g c) o -> c (g o)", g=GATES))
+            nc.scalar.dma_start(biou_sb[:], b_iou.rearrange("(g c) o -> c (g o)", g=GATES))
         nc.sync.dma_start(window[:], base)
         nc.sync.dma_start(offsets[:], offs)
 

@@ -13,6 +13,8 @@ S = 256
 GATE_I, GATE_O, GATE_U = 0, 1, 2
 GATES = 3
 PAIRS = 2
+PARTS = 4
+PART = N // PARTS
 BANK = 512
 
 FLOPS = 2 * (2 * H) * H * (K * N) + 2 * (2 * H) * (GATES * H) * N
@@ -118,20 +120,24 @@ def tile_improvedgraphlstmcell_kernel(
         iou_ps[GATE_O] = psum.tile([H, N], F32, name="o_ps", tag=f"neighbour{K - 1}")
         gate_products(GATE_O)
 
-        functions = {GATE_I: ACT.Sigmoid, GATE_O: ACT.Sigmoid, GATE_U: ACT.Tanh}
         gates = {}
         for g in (GATE_I, GATE_U, GATE_O):
             iou_pre = held.tile([H, N], F32, name=f"iou_pre{g}")
             nc.vector.tensor_tensor(iou_pre[:], iou_ps[g][:, 0:N], ioux_sb[:, g, :], ALU.add)
-            gates[g] = held.tile([H, N], F32, name=f"gate{g}")
-            nc.scalar.activation(gates[g][:], iou_pre[:], functions[g], bias=biou_sb[:, g : g + 1])
+            if g == GATE_U:
+                update_pre = iou_pre
+            else:
+                gates[g] = held.tile([H, N], F32, name=f"gate{g}")
+                nc.scalar.activation(gates[g][:], iou_pre[:], ACT.Sigmoid, bias=biou_sb[:, g : g + 1])
 
         tanh_cell = held.tile([H, N], F32, name="tanh_cell")
-        for half in range(2):
-            nodes = slice(half * N // 2, (half + 1) * N // 2)
-            iu = held.tile([H, N // 2], F32, name=f"iu{half}")
-            nc.vector.tensor_tensor(iu[:], gates[GATE_I][:, nodes], gates[GATE_U][:, nodes], ALU.mult)
-            cell = held.tile([H, N // 2], F32, name=f"cell{half}")
+        for part in range(PARTS):
+            nodes = slice(part * PART, (part + 1) * PART)
+            update = held.tile([H, PART], F32, name=f"update{part}")
+            nc.scalar.activation(update[:], update_pre[:, nodes], ACT.Tanh, bias=biou_sb[:, GATE_U : GATE_U + 1])
+            iu = held.tile([H, PART], F32, name=f"iu{part}")
+            nc.vector.tensor_tensor(iu[:], gates[GATE_I][:, nodes], update[:], ALU.mult)
+            cell = held.tile([H, PART], F32, name=f"cell{part}")
             nc.vector.tensor_tensor(cell[:], c_agg[:, nodes], iu[:], ALU.add)
             nc.scalar.activation(tanh_cell[:, nodes], cell[:], ACT.Tanh)
 

import concourse.mybir as mybir

F32 = mybir.dt.float32
BF16 = mybir.dt.bfloat16
U16 = mybir.dt.uint16
ALU = mybir.AluOpType
ACT = mybir.ActivationFunctionType

H = 128
K = 4
N = 128
S = 256
GATE_I, GATE_O, GATE_U = 0, 1, 2
GATES = 3
PAIRS = 2
PARTS = 4
PART = N // PARTS
BANK = 512

FLOPS = 2 * (2 * H) * H * (K * N) + 2 * (2 * H) * (GATES * H) * N


def tile_improvedgraphlstmcell_kernel(
    tc, base, h_mail, c_mail, lab, iou_x, wf_x, u_iou, u_f, b_iou, b_f, offs, out
):
    nc = tc.nc
    with (
        tc.tile_pool(name="held", bufs=1) as held,
        tc.psum_pool(name="psum", bufs=1) as psum,
    ):
        lab_rows = held.tile([H, 2 * K * N], BF16, name="lab_rows")
        h_all = held.tile([H, K * N], BF16, name="h_all")
        uf_sb = held.tile([H, 2, H], BF16, name="uf_sb")
        wfx_sb = held.tile([H, N], F32, name="wfx_sb")
        uiou_sb = held.tile([H, 2, GATES * H], BF16, name="uiou_sb")
        ioux_sb = held.tile([H, GATES, N], F32, name="ioux_sb")
        c_all = held.tile([H, K * N], F32, name="c_all")
        bf_sb = held.tile([H, 1], F32, name="bf_sb")
        biou_sb = held.tile([H, GATES], F32, name="biou_sb")
        window = held.tile([H, S], F32, name="window")
        offsets = held.tile([H, N // 16], U16, name="offsets")

        nc.scalar.dma_start(h_all[:], h_mail)
        nc.sync.dma_start(lab_rows[H - 1 : H, :], lab.bitcast(BF16))
        nc.gpsimd.memset(lab_rows[0 : H - 1, :].bitcast(F32), 0.0)
        nc.sync.dma_start(uf_sb[:], u_f.rearrange("(s d) c -> d s c", s=2))
        with nc.allow_non_contiguous_dma(reason="one bias value to a partition"):
            nc.scalar.dma_start(bf_sb[:], b_f)
        nc.sync.dma_start(wfx_sb[:], wf_x)
        nc.sync.dma_start(uiou_sb[:], u_iou.rearrange("(s d) r -> d s r", s=2))
        nc.sync.dma_start(c_all[:], c_mail)
        nc.sync.dma_start(ioux_sb[:], iou_x.rearrange("(g c) j -> c g j", g=GATES))
        with nc.allow_non_contiguous_dma(reason="one bias value to a partition"):
            nc.scalar.dma_start(biou_sb[:], b_iou.rearrange("(g c) o -> c (g o)", g=GATES))
        nc.sync.dma_start(window[:], base)
        nc.sync.dma_start(offsets[:], offs)

        zeros = held.tile([H, 1], F32, name="zeros")
        nc.vector.memset(zeros[:], 0.0)
        table_warmer = held.tile([H, 1], F32, name="table_warmer")
        nc.scalar.activation(table_warmer[:], zeros[:], ACT.Sigmoid)
        ones = held.tile([H, H], BF16, name="ones")
        nc.vector.memset(ones[:], 1.0)

        routed = [held.tile([H, 2, N], BF16, name=f"routed{k}") for k in range(K)]
        pair_sum = [held.tile([H, 2, N], BF16, name=f"pair_sum{p}") for p in range(PAIRS)]
        lab_ps = [psum.tile([H, N], BF16, name=f"lab_ps{k}", tag=f"neighbour{k}") for k in range(K)]
        for k in range(K):
            nc.tensor.matmul(
                lab_ps[k][:], ones[:], lab_rows[:, 2 * k * N + 1 : 2 * (k + 1) * N : 2], start=True, stop=True
            )
        for k in range(K):
            cols = slice(k * N, (k + 1) * N)
            h0, h1 = routed[k][:, 0, :], routed[k][:, 1, :]
            nc.vector.tensor_tensor(h1, h_all[:, cols], lab_ps[k][:], ALU.mult)
            nc.vector.tensor_tensor(h0, h_all[:, cols], h1, ALU.subtract)
            if k % 2 == 1:
                nc.vector.tensor_tensor(pair_sum[k // 2][:], routed[k - 1][:], routed[k][:], ALU.add)

        f_ps = [psum.tile([H, N], F32, name=f"f_ps{k}", tag=f"neighbour{k}") for k in range(K)]
        for k in range(K):
            for s in (1, 0):
                nc.tensor.matmul(
                    f_ps[k][:], uf_sb[:, s, :], routed[k][:, s, :], start=(s == 1), stop=(s == 0)
                )
        iou_ps = {
            GATE_I: psum.tile([H, BANK], F32, name="i_ps"),
            GATE_U: psum.tile([H, BANK], F32, name="u_ps"),
        }

        def gate_products(g):
            for p in range(PAIRS):
                for s in (1, 0):
                    nc.tensor.matmul(
                        iou_ps[g][:, 0:N],
                        uiou_sb[:, s, g * H : (g + 1) * H],
                        pair_sum[p][:, s, :],
                        start=(p == 0 and s == 1),
                        stop=(p == PAIRS - 1 and s == 0),
                    )

        gate_products(GATE_I)
        gate_products(GATE_U)

        c_agg = None
        for k in range(K):
            f_pre = held.tile([H, N], F32, name=f"f_pre{k}")
            nc.vector.tensor_tensor(f_pre[:], f_ps[k][:], wfx_sb[:], ALU.add)
            f_gate = held.tile([H, N], F32, name=f"f_gate{k}")
            nc.scalar.activation(f_gate[:], f_pre[:], ACT.Sigmoid, bias=bf_sb[:, 0:1])
            fc = held.tile([H, N], F32, name=f"fc{k}")
            nc.vector.tensor_tensor(fc[:], f_gate[:], c_all[:, k * N : (k + 1) * N], ALU.mult)
            if k == 0:
                c_agg = fc
            else:
                longer = held.tile([H, N], F32, name=f"c_agg{k}")
                nc.vector.tensor_tensor(longer[:], c_agg[:], fc[:], ALU.add)
                c_agg = longer

        iou_ps[GATE_O] = psum.tile([H, N], F32, name="o_ps", tag=f"neighbour{K - 1}")
        gate_products(GATE_O)

        gates = {}
        for g in (GATE_I, GATE_U, GATE_O):
            iou_pre = held.tile([H, N], F32, name=f"iou_pre{g}")
            nc.vector.tensor_tensor(iou_pre[:], iou_ps[g][:, 0:N], ioux_sb[:, g, :], ALU.add)
            if g == GATE_U:
                update_pre = iou_pre
            else:
                gates[g] = held.tile([H, N], F32, name=f"gate{g}")
                nc.scalar.activation(gates[g][:], iou_pre[:], ACT.Sigmoid, bias=biou_sb[:, g : g + 1])

        tanh_cell = held.tile([H, N], F32, name="tanh_cell")
        for part in range(PARTS):
            nodes = slice(part * PART, (part + 1) * PART)
            update = held.tile([H, PART], F32, name=f"update{part}")
            nc.scalar.activation(update[:], update_pre[:, nodes], ACT.Tanh, bias=biou_sb[:, GATE_U : GATE_U + 1])
            iu = held.tile([H, PART], F32, name=f"iu{part}")
            nc.vector.tensor_tensor(iu[:], gates[GATE_I][:, nodes], update[:], ALU.mult)
            cell = held.tile([H, PART], F32, name=f"cell{part}")
            nc.vector.tensor_tensor(cell[:], c_agg[:, nodes], iu[:], ALU.add)
            nc.scalar.activation(tanh_cell[:, nodes], cell[:], ACT.Tanh)

        nc.vector.tensor_tensor(
            window[:].indirect(offsets[:]), gates[GATE_O][:], tanh_cell[:], ALU.mult
        )
        nc.sync.dma_start(out, window[:])
